import numpy as np
import ml_dtypes


def mxq(x, axis, fmt="e4m3"):
    dtype, down = {"e4m3": (ml_dtypes.float8_e4m3fn, 7), "e5m2": (ml_dtypes.float8_e5m2, 14)}[fmt]
    v = np.moveaxis(np.asarray(x, np.float32).astype(ml_dtypes.bfloat16).astype(np.float64), axis, -1)
    blocks = v.reshape(v.shape[:-1] + (-1, 32))
    amax = np.abs(blocks).max(-1, keepdims=True)
    byte = np.maximum(np.where(amax > 0, np.frexp(amax)[1] - 1 + 127, 0) - down, 1)
    scale = np.exp2(byte - 127.0)
    codes = (blocks / scale).astype(np.float32).astype(dtype).astype(np.float64)
    return np.moveaxis((codes * scale).reshape(v.shape), -1, axis)


WIDE = False


def mx_kscale(k):
    if not WIDE:
        return np.ones(k)
    levels = np.array([10, -10, 5, -5, 0])
    if k % 512:
        return np.exp2(np.random.permutation(np.resize(levels, k // 32))).repeat(32)
    a = np.empty((k // 512, 16))
    for p in range(k // 512):
        a[p, :8] = np.random.permutation(np.resize(levels, 8))
        for g in range(8):
            far = levels[np.abs(levels - a[p, g]) >= 10]
            a[p, g + 8] = far[np.random.randint(len(far))]
    return np.exp2(a.ravel()).repeat(32)


BF16 = ml_dtypes.bfloat16


def bf(x):
    return np.asarray(x, np.float32).astype(BF16)


def f64(x):
    return np.asarray(x).astype(np.float64)


N, C, E, T, H, CK = 3, 512, 512, 1024, 8, 64
EPS = 1e-5


def setup_inputs():
    s = mx_kscale(C)
    return {
        "h_attn": bf(np.random.standard_normal((N, T, C)) * 0.4 * s),
        "x": bf(np.random.standard_normal((N, E, T))),
        "masks": bf(np.random.uniform(0.2, 1.0, (N, 1, T))),
        "Wo": bf(np.random.standard_normal((E, C)) * 2.0 / np.sqrt(C) / s[None, :]),
        "bo": bf(np.random.standard_normal(E) * 0.5),
    }


def reference(h_attn, x, masks, Wo, bo):
    o = (mxq(f64(h_attn), 2, "e4m3") @ mxq(f64(Wo), 1, "e4m3").T) + f64(bo)
    y = o.transpose(0, 2, 1) * f64(masks) + f64(x)
    mean = y.mean(-1, keepdims=True)
    var = np.square(y - mean).mean(-1, keepdims=True)
    return (y - mean) / np.sqrt(var + EPS)

@@ -1,0 +1,260 @@
+from contextlib import ExitStack
+
+import concourse.mybir as mybir
+from concourse.masks import make_identity
+
+F32 = mybir.dt.float32
+BF16 = mybir.dt.bfloat16
+U32 = mybir.dt.uint32
+U8 = mybir.dt.uint8
+FP8X4 = mybir.dt.float8_e4m3fn_x4
+ALU = mybir.AluOpType
+ACT = mybir.ActivationFunctionType
+
+P = 128
+SEQS = 3
+FRAMES = 1024
+CHANNELS = 512
+GROUPS = CHANNELS // P
+PACK = 4
+BANK = 512
+HALVES = FRAMES // BANK
+EPS = 1e-5
+SLABS = SEQS * GROUPS
+VECTOR_COLS = 128
+DRAIN_VECTOR_COLS = 640
+
+FLOPS = 2 * SEQS * FRAMES * CHANNELS * CHANNELS
+
+
+def tile_transformerencoderblock_pa_kernel(tc, h_attn, x, masks, Wo, bo, out):
+    nc = tc.nc
+    with ExitStack() as ctx:
+        consts = ctx.enter_context(tc.tile_pool(name="consts", bufs=1))
+        inputs = ctx.enter_context(tc.tile_pool(name="inputs", bufs=1))
+        quant = ctx.enter_context(tc.tile_pool(name="quant", bufs=SEQS))
+        scratch = ctx.enter_context(tc.tile_pool(name="scratch", bufs=3))
+        slabs = ctx.enter_context(tc.tile_pool(name="slabs", bufs=4))
+        stats = ctx.enter_context(tc.tile_pool(name="stats", bufs=4))
+        transposed_psum = ctx.enter_context(tc.psum_pool(name="transposed_psum", bufs=3))
+        mask_psum = ctx.enter_context(tc.psum_pool(name="mask_psum", bufs=1))
+        product_psum = ctx.enter_context(tc.psum_pool(name="product_psum", bufs=4))
+        ctx.enter_context(tc.manual_schedule())
+
+        h_view = h_attn.rearrange("n (j r i) c -> n r j (i c)", r=P, i=2)
+        x_view = x.rearrange("n (p a) t -> n p a t", a=GROUPS)
+        out_view = out.rearrange("n (p a) t -> n p a t", a=GROUPS)
+
+        ident = consts.tile([P, P], F32)
+        make_identity(nc, ident[:])
+        minus_half = consts.tile([P, 1], F32)
+        nc.gpsimd.memset(minus_half[:], -0.5)
+        mask_rows = consts.tile([P, SEQS * FRAMES], BF16)
+        nc.vector.memset(mask_rows[:], 0.0)
+        ones = consts.tile([P, P], BF16)
+        nc.vector.memset(ones[:], 1.0)
+        mask_sb = consts.tile([P, SEQS * FRAMES], BF16)
+
+        w_sb = consts.tile([P, GROUPS * CHANNELS], BF16)
+        bo_sb = consts.tile([P, GROUPS], BF16)
+        h_sb = [
+            inputs.tile([P, FRAMES * CHANNELS // P], BF16, name="h_sb%d" % n) for n in range(SEQS)
+        ]
+        x_sb = [inputs.tile([P, GROUPS, FRAMES], BF16, name="x_sb%d" % n) for n in range(SEQS)]
+
+        def load_frames(n, half):
+            nc.sync.dma_start(
+                out=h_sb[n][:, half * 2048 : (half + 1) * 2048].rearrange("r (j c) -> r j c", j=2),
+                in_=h_view[n][:, 2 * half : 2 * half + 2, :],
+            )
+
+        nc.sync.dma_start(out=w_sb[:], in_=Wo.rearrange("(p a) c -> p (a c)", a=GROUPS))
+        load_frames(0, 0)
+        nc.sync.dma_start(out=mask_rows[0:1, :], in_=masks.rearrange("n o t -> o (n t)"))
+        nc.sync.dma_start(out=bo_sb[:], in_=bo.rearrange("(p a) -> p a", a=GROUPS))
+        load_frames(0, 1)
+        nc.sync.dma_start(out=x_sb[0][:], in_=x_view[0])
+        for n in range(1, SEQS):
+            load_frames(n, 0)
+            load_frames(n, 1)
+        for n in range(1, SEQS):
+            nc.sync.dma_start(out=x_sb[n][:], in_=x_view[n])
+
+        def broadcast_mask(n):
+            mask_ps = mask_psum.tile([P, FRAMES], BF16)
+            for half in range(HALVES):
+                nc.tensor.matmul(
+                    out=mask_ps[:, half * BANK : (half + 1) * BANK],
+                    lhsT=ones[:],
+                    rhs=mask_rows[:, n * FRAMES + half * BANK : n * FRAMES + (half + 1) * BANK],
+                    start=True,
+                    stop=True,
+                )
+            nc.scalar.copy(out=mask_sb[:, n * FRAMES : (n + 1) * FRAMES], in_=mask_ps[:])
+
+        w_words = w_sb[:].bitcast(F32)
+        w_grouped = consts.tile([P, GROUPS * P * PACK], BF16, align_bytes=64)
+        w_grouped_words = w_grouped[:].bitcast(F32)
+        w_codes = consts.tile([P, GROUPS * P], U32, align_bytes=64)
+        w_scales = consts.tile([P, GROUPS * P], U8, align_bytes=64)
+        for pair in range(GROUPS // 2):
+            w_ps = transposed_psum.tile([P, 2, 2, P], F32, tag="transposed")
+            for a2 in range(2):
+                for u in range(2):
+                    row = (2 * pair + a2) * 256
+                    nc.tensor.transpose(
+                        w_ps[:, a2, u, :], w_words[:, row + u : row + 256 : 2], ident[:]
+                    )
+            regrouped = w_grouped_words[:, pair * BANK : (pair + 1) * BANK].rearrange(
+                "q (a p u) -> q a p u", a=2, u=2
+            )
+            if pair == 0:
+                nc.vector.tensor_copy(out=regrouped, in_=w_ps[:].rearrange("q a u p -> q a p u"))
+            else:
+                nc.scalar.copy(out=regrouped, in_=w_ps[:].rearrange("q a u p -> q a p u"))
+        nc.vector.quantize_mx(
+            out=w_codes[:].bitcast(FP8X4), scales=w_scales[:], in_=w_grouped[:]
+        )
+
+        frames = {}
+
+        def transpose_quarter(n, j, on_vector=False):
+            if j == 0:
+                h_grouped = quant.tile([P, FRAMES * PACK], BF16, align_bytes=64)
+                h_codes = quant.tile([P, FRAMES], U32, align_bytes=64)
+                h_scales = quant.tile([P, FRAMES], U8, align_bytes=64)
+                frames[n] = (h_grouped, h_codes, h_scales)
+            h_words = h_sb[n][:].bitcast(F32)
+            h_ps = transposed_psum.tile([P, 2, 2, P], F32, tag="transposed")
+            for i in range(2):
+                for u in range(2):
+                    row = j * 512 + i * 256
+                    nc.tensor.transpose(
+                        h_ps[:, i, u, :], h_words[:, row + u : row + 256 : 2], ident[:]
+                    )
+            regrouped = frames[n][0][:].bitcast(F32)[:, j * BANK : (j + 1) * BANK].rearrange(
+                "q (r i u) -> q r i u", i=2, u=2
+            )
+            if on_vector:
+                nc.vector.tensor_copy(out=regrouped, in_=h_ps[:].rearrange("q i u r -> q r i u"))
+            else:
+                nc.scalar.copy(out=regrouped, in_=h_ps[:].rearrange("q i u r -> q r i u"))
+
+        def quantise_half(n, half):
+            h_grouped, h_codes, h_scales = frames[n]
+            nc.vector.quantize_mx(
+                out=h_codes[:, half * BANK : (half + 1) * BANK].bitcast(FP8X4),
+                scales=h_scales[:, half * BANK : (half + 1) * BANK],
+                in_=h_grouped[:, half * BANK * PACK : (half + 1) * BANK * PACK],
+            )
+
+        projected = {}
+        summed = {}
+        scaled = {}
+
+        def project(k):
+            n, a = divmod(k, GROUPS)
+            h_codes, h_scales = frames[n][1:]
+            masked = scratch.tile([P, FRAMES], F32)
+            for half in range(HALVES):
+                cols = slice(half * BANK, (half + 1) * BANK)
+                product = product_psum.tile([P, BANK], F32)
+                nc.tensor.matmul_mx(
+                    out=product[:],
+                    lhsT=w_codes[:, a * P : (a + 1) * P].bitcast(FP8X4),
+                    lhsT_scale=w_scales[:, a * P : (a + 1) * P],
+                    rhs=h_codes[:, cols].bitcast(FP8X4),
+                    rhs_scale=h_scales[:, cols],
+                    start=True,
+                    stop=True,
+                )
+                nc.vector.scalar_tensor_tensor(
+                    out=masked[:, cols],
+                    in0=product[:],
+                    scalar=bias_f32[:, a : a + 1],
+                    in1=mask_sb[:, n * FRAMES + half * BANK : n * FRAMES + (half + 1) * BANK],
+                    op0=ALU.add,
+                    op1=ALU.mult,
+                )
+            projected[k] = masked
+
+        def add_residual(k):
+            n, a = divmod(k, GROUPS)
+            masked = projected[k]
+            y = slabs.tile([P, FRAMES], F32)
+            y_sum = stats.tile([P, 1], F32)
+            nc.vector.scalar_tensor_tensor(
+                out=y[:],
+                in0=masked[:],
+                scalar=1.0,
+                in1=x_sb[n][:, a, :],
+                op0=ALU.mult,
+                op1=ALU.add,
+                accum_out=y_sum[:],
+            )
+            summed[k] = (y, y_sum)
+
+        def deviation(k):
+            y, y_sum = summed[k]
+            squares = scratch.tile([P, FRAMES], BF16)
+            dev_sum = stats.tile([P, 1], F32)
+            nc.scalar.activation(
+                out=squares[:], in_=y[:], func=ACT.Square, bias=y_sum[:], scale=-float(FRAMES),
+                accum_out=dev_sum[:],
+            )
+            var_eps = stats.tile([P, 1], F32)
+            nc.gpsimd.tensor_scalar(
+                out=var_eps[:], in0=dev_sum[:], scalar1=1.0 / FRAMES**3, scalar2=EPS,
+                op0=ALU.mult, op1=ALU.add,
+            )
+            rstd = stats.tile([P, 1], F32)
+            nc.gpsimd.tensor_tensor(out=rstd[:], in0=var_eps[:], in1=minus_half[:], op=ALU.pow)
+            shift = stats.tile([P, 1], F32)
+            nc.gpsimd.tensor_scalar(
+                out=shift[:], in0=y_sum[:], scalar1=rstd[:], scalar2=-1.0 / FRAMES,
+                op0=ALU.mult, op1=ALU.mult,
+            )
+            scaled[k] = (rstd, shift)
+
+        def normalise_and_store(k, vector_cols):
+            n, a = divmod(k, GROUPS)
+            y = summed[k][0]
+            rstd, shift = scaled[k]
+            normed = slabs.tile([P, FRAMES], F32)
+            split = FRAMES - vector_cols
+            nc.scalar.activation(
+                out=normed[:, :split], in_=y[:, :split], func=ACT.Identity,
+                bias=shift[:], scale=rstd[:],
+            )
+            nc.vector.tensor_scalar(
+                out=normed[:, split:], in0=y[:, split:], scalar1=rstd[:], scalar2=shift[:],
+                op0=ALU.mult, op1=ALU.add,
+            )
+            nc.sync.dma_start(out=out_view[n][:, a, :], in_=normed[:])
+
+        for j in range(GROUPS):
+            transpose_quarter(0, j, on_vector=(j % 2 == 1))
+            if j % 2 == 1:
+                quantise_half(0, j // 2)
+        broadcast_mask(0)
+        bias_f32 = consts.tile([P, GROUPS], F32)
+        nc.vector.tensor_copy(out=bias_f32[:], in_=bo_sb[:])
+
+        for k in range(SLABS + 3):
+            if 2 <= k < SLABS + 2:
+                deviation(k - 2)
+            if k < SLABS:
+                project(k)
+            if 1 <= k < SLABS + 1:
+                add_residual(k - 1)
+            if 1 <= k <= (SEQS - 1) * HALVES:
+                n, half = divmod(k + 1, HALVES)
+                transpose_quarter(n, 2 * half)
+                transpose_quarter(n, 2 * half + 1)
+            if 2 <= k <= (SEQS - 1) * HALVES + 1:
+                n, half = divmod(k, HALVES)
+                quantise_half(n, half)
+            if 1 <= k < SEQS:
+                broadcast_mask(k)
+            if k >= 3:
+                normalise_and_store(k - 3, VECTOR_COLS if k <= SLABS else DRAIN_VECTOR_COLS)

@@ -21,7 +21,7 @@ BANK = 512
 HALVES = FRAMES // BANK
 EPS = 1e-5
 SLABS = SEQS * GROUPS
-VECTOR_COLS = 128
+VECTOR_COLS = 0
 DRAIN_VECTOR_COLS = 640
 
 FLOPS = 2 * SEQS * FRAMES * CHANNELS * CHANNELS
@@ -36,8 +36,7 @@ def tile_transformerencoderblock_pa_kernel(tc, h_attn, x, masks, Wo, bo, out):
         scratch = ctx.enter_context(tc.tile_pool(name="scratch", bufs=3))
         slabs = ctx.enter_context(tc.tile_pool(name="slabs", bufs=4))
         stats = ctx.enter_context(tc.tile_pool(name="stats", bufs=4))
-        transposed_psum = ctx.enter_context(tc.psum_pool(name="transposed_psum", bufs=3))
-        mask_psum = ctx.enter_context(tc.psum_pool(name="mask_psum", bufs=1))
+        transposed_psum = ctx.enter_context(tc.psum_pool(name="transposed_psum", bufs=4))
         product_psum = ctx.enter_context(tc.psum_pool(name="product_psum", bufs=4))
         ctx.enter_context(tc.manual_schedule())
 
@@ -45,14 +44,14 @@ def tile_transformerencoderblock_pa_kernel(tc, h_attn, x, masks, Wo, bo, out):
         x_view = x.rearrange("n (p a) t -> n p a t", a=GROUPS)
         out_view = out.rearrange("n (p a) t -> n p a t", a=GROUPS)
 
+        mask_rows = consts.tile([P, FRAMES], BF16)
+        nc.vector.memset(mask_rows[:].bitcast(U32), 0)
         ident = consts.tile([P, P], F32)
         make_identity(nc, ident[:])
         minus_half = consts.tile([P, 1], F32)
         nc.gpsimd.memset(minus_half[:], -0.5)
-        mask_rows = consts.tile([P, SEQS * FRAMES], BF16)
-        nc.vector.memset(mask_rows[:], 0.0)
-        ones = consts.tile([P, P], BF16)
-        nc.vector.memset(ones[:], 1.0)
+        row_select = consts.tile([P, SEQS], BF16)
+        nc.vector.tensor_copy(out=row_select[:], in_=ident[:, :SEQS])
         mask_sb = consts.tile([P, SEQS * FRAMES], BF16)
 
         w_sb = consts.tile([P, GROUPS * CHANNELS], BF16)
@@ -62,42 +61,64 @@ def tile_transformerencoderblock_pa_kernel(tc, h_attn, x, masks, Wo, bo, out):
         ]
         x_sb = [inputs.tile([P, GROUPS, FRAMES], BF16, name="x_sb%d" % n) for n in range(SEQS)]
 
-        def load_frames(n, half):
+        def load_frames(n, first, count):
             nc.sync.dma_start(
-                out=h_sb[n][:, half * 2048 : (half + 1) * 2048].rearrange("r (j c) -> r j c", j=2),
-                in_=h_view[n][:, 2 * half : 2 * half + 2, :],
+                out=h_sb[n][:, first * 1024 : (first + count) * 1024].rearrange(
+                    "r (j c) -> r j c", j=count
+                ),
+                in_=h_view[n][:, first : first + count, :],
             )
 
-        nc.sync.dma_start(out=w_sb[:], in_=Wo.rearrange("(p a) c -> p (a c)", a=GROUPS))
-        load_frames(0, 0)
-        nc.sync.dma_start(out=mask_rows[0:1, :], in_=masks.rearrange("n o t -> o (n t)"))
-        nc.sync.dma_start(out=bo_sb[:], in_=bo.rearrange("(p a) -> p a", a=GROUPS))
-        load_frames(0, 1)
-        nc.sync.dma_start(out=x_sb[0][:], in_=x_view[0])
-        for n in range(1, SEQS):
-            load_frames(n, 0)
-            load_frames(n, 1)
+        def load_weights(pair):
+            nc.sync.dma_start(
+                out=w_sb[:, pair * 1024 : (pair + 1) * 1024],
+                in_=Wo.rearrange("(p a) c -> p (a c)", a=GROUPS)[:, pair * 1024 : (pair + 1) * 1024],
+            )
+
+        def load_residual(n, pair):
+            groups = slice(2 * pair, 2 * pair + 2)
+            nc.sync.dma_start(out=x_sb[n][:, groups, :], in_=x_view[n][:, groups, :])
+
+        mask_view = masks.rearrange("n o t -> (n o) t")
+        nc.scalar.dma_start(out=mask_rows[0:1, :], in_=mask_view[0:1, :])
+        nc.scalar.dma_start(out=mask_rows[1:SEQS, :], in_=mask_view[1:SEQS, :])
+        nc.scalar.dma_start(out=bo_sb[:], in_=bo.rearrange("(p a) -> p a", a=GROUPS))
+        load_weights(0)
+        load_frames(0, 0, 1)
+        load_frames(0, 1, 1)
+        load_frames(0, 2, 2)
+        load_weights(1)
+        load_frames(1, 0, 2)
+        load_residual(0, 0)
+        load_frames(1, 2, 2)
+        load_frames(2, 0, 2)
+        load_residual(0, 1)
+        load_frames(2, 2, 2)
         for n in range(1, SEQS):
             nc.sync.dma_start(out=x_sb[n][:], in_=x_view[n])
 
-        def broadcast_mask(n):
-            mask_ps = mask_psum.tile([P, FRAMES], BF16)
-            for half in range(HALVES):
+        def broadcast_mask(n, halves=(0, 1)):
+            mask_ps = transposed_psum.tile([P, FRAMES], BF16, tag="transposed")
+            for half in halves:
                 nc.tensor.matmul(
                     out=mask_ps[:, half * BANK : (half + 1) * BANK],
-                    lhsT=ones[:],
-                    rhs=mask_rows[:, n * FRAMES + half * BANK : n * FRAMES + (half + 1) * BANK],
+                    lhsT=row_select[:, n : n + 1].to_broadcast([P, P]),
+                    rhs=mask_rows[:, half * BANK : (half + 1) * BANK],
                     start=True,
                     stop=True,
                 )
-            nc.scalar.copy(out=mask_sb[:, n * FRAMES : (n + 1) * FRAMES], in_=mask_ps[:])
+            first, end = halves[0] * BANK, (halves[-1] + 1) * BANK
+            nc.scalar.copy(
+                out=mask_sb[:, n * FRAMES + first : n * FRAMES + end], in_=mask_ps[:, first:end]
+            )
 
         w_words = w_sb[:].bitcast(F32)
         w_grouped = consts.tile([P, GROUPS * P * PACK], BF16, align_bytes=64)
         w_grouped_words = w_grouped[:].bitcast(F32)
         w_codes = consts.tile([P, GROUPS * P], U32, align_bytes=64)
         w_scales = consts.tile([P, GROUPS * P], U8, align_bytes=64)
-        for pair in range(GROUPS // 2):
+
+        def transpose_weights(pair):
             w_ps = transposed_psum.tile([P, 2, 2, P], F32, tag="transposed")
             for a2 in range(2):
                 for u in range(2):
@@ -108,13 +129,15 @@ def tile_transformerencoderblock_pa_kernel(tc, h_attn, x, masks, Wo, bo, out):
             regrouped = w_grouped_words[:, pair * BANK : (pair + 1) * BANK].rearrange(
                 "q (a p u) -> q a p u", a=2, u=2
             )
-            if pair == 0:
-                nc.vector.tensor_copy(out=regrouped, in_=w_ps[:].rearrange("q a u p -> q a p u"))
-            else:
-                nc.scalar.copy(out=regrouped, in_=w_ps[:].rearrange("q a u p -> q a p u"))
-        nc.vector.quantize_mx(
-            out=w_codes[:].bitcast(FP8X4), scales=w_scales[:], in_=w_grouped[:]
-        )
+            nc.scalar.copy(out=regrouped, in_=w_ps[:].rearrange("q a u p -> q a p u"))
+
+        def quantise_weights(pair):
+            cols = slice(2 * pair * P, (2 * pair + 2) * P)
+            nc.vector.quantize_mx(
+                out=w_codes[:, cols].bitcast(FP8X4),
+                scales=w_scales[:, cols],
+                in_=w_grouped[:, pair * 1024 : (pair + 1) * 1024],
+            )
 
         frames = {}
 
@@ -152,11 +175,13 @@ def tile_transformerencoderblock_pa_kernel(tc, h_attn, x, masks, Wo, bo, out):
         summed = {}
         scaled = {}
 
-        def project(k):
+        def project(k, halves=(0, 1)):
             n, a = divmod(k, GROUPS)
             h_codes, h_scales = frames[n][1:]
-            masked = scratch.tile([P, FRAMES], F32)
-            for half in range(HALVES):
+            if halves[0] == 0:
+                projected[k] = scratch.tile([P, FRAMES], F32, name="masked")
+            masked = projected[k]
+            for half in halves:
                 cols = slice(half * BANK, (half + 1) * BANK)
                 product = product_psum.tile([P, BANK], F32)
                 nc.tensor.matmul_mx(
@@ -176,7 +201,6 @@ def tile_transformerencoderblock_pa_kernel(tc, h_attn, x, masks, Wo, bo, out):
                     op0=ALU.add,
                     op1=ALU.mult,
                 )
-            projected[k] = masked
 
         def add_residual(k):
             n, a = divmod(k, GROUPS)
@@ -222,39 +246,62 @@ def tile_transformerencoderblock_pa_kernel(tc, h_attn, x, masks, Wo, bo, out):
             rstd, shift = scaled[k]
             normed = slabs.tile([P, FRAMES], F32)
             split = FRAMES - vector_cols
-            nc.scalar.activation(
-                out=normed[:, :split], in_=y[:, :split], func=ACT.Identity,
-                bias=shift[:], scale=rstd[:],
-            )
-            nc.vector.tensor_scalar(
-                out=normed[:, split:], in0=y[:, split:], scalar1=rstd[:], scalar2=shift[:],
-                op0=ALU.mult, op1=ALU.add,
-            )
+            if split > 0:
+                nc.scalar.activation(
+                    out=normed[:, :split], in_=y[:, :split], func=ACT.Identity,
+                    bias=shift[:], scale=rstd[:],
+                )
+            if vector_cols > 0:
+                nc.vector.tensor_scalar(
+                    out=normed[:, split:], in0=y[:, split:], scalar1=rstd[:], scalar2=shift[:],
+                    op0=ALU.mult, op1=ALU.add,
+                )
             nc.sync.dma_start(out=out_view[n][:, a, :], in_=normed[:])
 
-        for j in range(GROUPS):
-            transpose_quarter(0, j, on_vector=(j % 2 == 1))
-            if j % 2 == 1:
-                quantise_half(0, j // 2)
-        broadcast_mask(0)
         bias_f32 = consts.tile([P, GROUPS], F32)
-        nc.vector.tensor_copy(out=bias_f32[:], in_=bo_sb[:])
+        nc.gpsimd.tensor_copy(out=bias_f32[:], in_=bo_sb[:])
 
-        for k in range(SLABS + 3):
-            if 2 <= k < SLABS + 2:
-                deviation(k - 2)
-            if k < SLABS:
-                project(k)
-            if 1 <= k < SLABS + 1:
-                add_residual(k - 1)
-            if 1 <= k <= (SEQS - 1) * HALVES:
+        transpose_weights(0)
+        transpose_quarter(0, 0, on_vector=True)
+        transpose_quarter(0, 1)
+        quantise_weights(0)
+        quantise_half(0, 0)
+        broadcast_mask(0, (0,))
+        transpose_quarter(0, 2)
+        transpose_quarter(0, 3)
+        project(0, (0,))
+        project(1, (0,))
+        broadcast_mask(0, (1,))
+        transpose_weights(1)
+        transpose_quarter(1, 0)
+        transpose_quarter(1, 1)
+        quantise_half(0, 1)
+        quantise_weights(1)
+        project(0, (1,))
+        project(1, (1,))
+        add_residual(0)
+
+        for k in range(2, SLABS):
+            if k <= 4:
                 n, half = divmod(k + 1, HALVES)
                 transpose_quarter(n, 2 * half)
                 transpose_quarter(n, 2 * half + 1)
-            if 2 <= k <= (SEQS - 1) * HALVES + 1:
-                n, half = divmod(k, HALVES)
-                quantise_half(n, half)
-            if 1 <= k < SEQS:
-                broadcast_mask(k)
+            if k == 2:
+                broadcast_mask(1)
+            if k == 5:
+                broadcast_mask(2)
+            deviation(k - 2)
+            if k % GROUPS == 3 and k < SLABS - 1:
+                quantise_half(k // GROUPS + 1, 0)
+            if k % GROUPS == 0:
+                quantise_half(k // GROUPS, 1)
+            project(k)
+            add_residual(k - 1)
             if k >= 3:
-                normalise_and_store(k - 3, VECTOR_COLS if k <= SLABS else DRAIN_VECTOR_COLS)
+                normalise_and_store(k - 3, VECTOR_COLS)
+        deviation(SLABS - 2)
+        add_residual(SLABS - 1)
+        normalise_and_store(SLABS - 3, FRAMES)
+        deviation(SLABS - 1)
+        normalise_and_store(SLABS - 2, DRAIN_VECTOR_COLS)
+        normalise_and_store(SLABS - 1, DRAIN_VECTOR_COLS)

@@ -48,8 +48,9 @@ def tile_transformerencoderblock_pa_kernel(tc, h_attn, x, masks, Wo, bo, out):
         nc.vector.memset(mask_rows[:].bitcast(U32), 0)
         ident = consts.tile([P, P], F32)
         make_identity(nc, ident[:])
-        minus_half = consts.tile([P, 1], F32)
-        nc.gpsimd.memset(minus_half[:], -0.5)
+        warm = consts.tile([P, 1], F32)
+        eps = consts.tile([P, 1], F32)
+        nc.gpsimd.memset(eps[:], EPS)
         row_select = consts.tile([P, SEQS], BF16)
         nc.vector.tensor_copy(out=row_select[:], in_=ident[:, :SEQS])
         mask_sb = consts.tile([P, SEQS * FRAMES], BF16)
@@ -96,6 +97,10 @@ def tile_transformerencoderblock_pa_kernel(tc, h_attn, x, masks, Wo, bo, out):
         load_frames(2, 2, 2)
         for n in range(1, SEQS):
             nc.sync.dma_start(out=x_sb[n][:], in_=x_view[n])
+
+        nc.scalar.activation(
+            out=warm[:], in_=eps[:], func=ACT.Abs_reciprocal_sqrt, bias=eps[:], scale=1.0
+        )
 
         def broadcast_mask(n, halves=(0, 1)):
             mask_ps = transposed_psum.tile([P, FRAMES], BF16, tag="transposed")
@@ -173,7 +178,10 @@ def tile_transformerencoderblock_pa_kernel(tc, h_attn, x, masks, Wo, bo, out):
 
         projected = {}
         summed = {}
-        scaled = {}
+        deviations = {}
+        inverted = {}
+        shifts = {}
+        minus_means = {}
 
         def project(k, halves=(0, 1)):
             n, a = divmod(k, GROUPS)
@@ -226,37 +234,52 @@ def tile_transformerencoderblock_pa_kernel(tc, h_attn, x, masks, Wo, bo, out):
                 out=squares[:], in_=y[:], func=ACT.Square, bias=y_sum[:], scale=-float(FRAMES),
                 accum_out=dev_sum[:],
             )
-            var_eps = stats.tile([P, 1], F32)
-            nc.gpsimd.tensor_scalar(
-                out=var_eps[:], in0=dev_sum[:], scalar1=1.0 / FRAMES**3, scalar2=EPS,
-                op0=ALU.mult, op1=ALU.add,
-            )
-            rstd = stats.tile([P, 1], F32)
-            nc.gpsimd.tensor_tensor(out=rstd[:], in0=var_eps[:], in1=minus_half[:], op=ALU.pow)
-            shift = stats.tile([P, 1], F32)
-            nc.gpsimd.tensor_scalar(
-                out=shift[:], in0=y_sum[:], scalar1=rstd[:], scalar2=-1.0 / FRAMES,
-                op0=ALU.mult, op1=ALU.mult,
-            )
-            scaled[k] = (rstd, shift)
+            deviations[k] = dev_sum
 
-        def normalise_and_store(k, vector_cols):
+        def invert_deviation(k):
+            rstd = stats.tile([P, 1], F32)
+            nc.scalar.activation(
+                out=rstd[:], in_=deviations[k][:], func=ACT.Abs_reciprocal_sqrt,
+                bias=eps[:], scale=1.0 / FRAMES**3,
+            )
+            inverted[k] = rstd
+
+        def store(k, cols, normed):
             n, a = divmod(k, GROUPS)
-            y = summed[k][0]
-            rstd, shift = scaled[k]
+            nc.sync.dma_start(out=out_view[n][:, a, cols], in_=normed[:, cols])
+
+        def shift_mean(k):
+            shift = stats.tile([P, 1], F32)
+            nc.scalar.activation(
+                out=shift[:], in_=minus_means[k][:], func=ACT.Identity, scale=inverted[k][:]
+            )
+            shifts[k] = shift
+
+        def normalise_on_scalar(k):
             normed = slabs.tile([P, FRAMES], F32)
-            split = FRAMES - vector_cols
-            if split > 0:
-                nc.scalar.activation(
-                    out=normed[:, :split], in_=y[:, :split], func=ACT.Identity,
-                    bias=shift[:], scale=rstd[:],
-                )
-            if vector_cols > 0:
+            nc.scalar.activation(
+                out=normed[:], in_=summed[k][0][:], func=ACT.Identity,
+                bias=shifts[k][:], scale=inverted[k][:],
+            )
+            store(k, slice(0, FRAMES), normed)
+
+        def minus_mean(k):
+            minus_means[k] = stats.tile([P, 1], F32, name="minus_mean")
+            nc.vector.tensor_scalar(
+                out=minus_means[k][:], in0=summed[k][1][:], scalar1=-1.0 / FRAMES, scalar2=None,
+                op0=ALU.mult,
+            )
+
+        def normalise_on_vector(k, pieces=1):
+            normed = slabs.tile([P, FRAMES], F32)
+            width = FRAMES // pieces
+            for i in range(pieces):
+                cols = slice(i * width, (i + 1) * width)
                 nc.vector.tensor_scalar(
-                    out=normed[:, split:], in0=y[:, split:], scalar1=rstd[:], scalar2=shift[:],
-                    op0=ALU.mult, op1=ALU.add,
+                    out=normed[:, cols], in0=summed[k][0][:, cols], scalar1=minus_means[k][:],
+                    scalar2=inverted[k][:], op0=ALU.add, op1=ALU.mult,
                 )
-            nc.sync.dma_start(out=out_view[n][:, a, :], in_=normed[:])
+                store(k, cols, normed)
 
         bias_f32 = consts.tile([P, GROUPS], F32)
         nc.gpsimd.tensor_copy(out=bias_f32[:], in_=bo_sb[:])
@@ -291,17 +314,28 @@ def tile_transformerencoderblock_pa_kernel(tc, h_attn, x, masks, Wo, bo, out):
             if k == 5:
                 broadcast_mask(2)
             deviation(k - 2)
+            on_vector = (k - 3) % GROUPS == GROUPS - 1
+            if k >= 3 and not on_vector:
+                shift_mean(k - 3)
+            invert_deviation(k - 2)
+            if k >= 3 and not on_vector:
+                normalise_on_scalar(k - 3)
             if k % GROUPS == 3 and k < SLABS - 1:
                 quantise_half(k // GROUPS + 1, 0)
             if k % GROUPS == 0:
                 quantise_half(k // GROUPS, 1)
             project(k)
+            minus_mean(k - 2)
             add_residual(k - 1)
-            if k >= 3:
-                normalise_and_store(k - 3, VECTOR_COLS)
+            if k >= 3 and on_vector:
+                normalise_on_vector(k - 3)
         deviation(SLABS - 2)
+        invert_deviation(SLABS - 2)
         add_residual(SLABS - 1)
-        normalise_and_store(SLABS - 3, FRAMES)
         deviation(SLABS - 1)
-        normalise_and_store(SLABS - 2, DRAIN_VECTOR_COLS)
-        normalise_and_store(SLABS - 1, DRAIN_VECTOR_COLS)
+        invert_deviation(SLABS - 1)
+        minus_mean(SLABS - 2)
+        normalise_on_vector(SLABS - 3)
+        minus_mean(SLABS - 1)
+        normalise_on_vector(SLABS - 2)
+        normalise_on_vector(SLABS - 1, pieces=2)

@@ -263,6 +263,19 @@ def tile_transformerencoderblock_pa_kernel(tc, h_attn, x, masks, Wo, bo, out):
             )
             store(k, slice(0, FRAMES), normed)
 
+        def normalise_on_gpsimd(k):
+            shift = stats.tile([P, 1], F32)
+            nc.vector.tensor_scalar(
+                out=shift[:], in0=summed[k][1][:], scalar1=inverted[k][:], scalar2=-1.0 / FRAMES,
+                op0=ALU.mult, op1=ALU.mult,
+            )
+            normed = slabs.tile([P, FRAMES], F32)
+            nc.gpsimd.tensor_scalar(
+                out=normed[:], in0=summed[k][0][:], scalar1=inverted[k][:], scalar2=shift[:],
+                op0=ALU.mult, op1=ALU.add,
+            )
+            store(k, slice(0, FRAMES), normed)
+
         def minus_mean(k):
             minus_means[k] = stats.tile([P, 1], F32, name="minus_mean")
             nc.vector.tensor_scalar(
@@ -314,21 +327,22 @@ def tile_transformerencoderblock_pa_kernel(tc, h_attn, x, masks, Wo, bo, out):
             if k == 5:
                 broadcast_mask(2)
             deviation(k - 2)
-            on_vector = (k - 3) % GROUPS == GROUPS - 1
-            if k >= 3 and not on_vector:
+            on_gpsimd = (k - 3) % 2 == 1
+            if k >= 3 and not on_gpsimd:
                 shift_mean(k - 3)
             invert_deviation(k - 2)
-            if k >= 3 and not on_vector:
+            if k >= 3 and not on_gpsimd:
                 normalise_on_scalar(k - 3)
             if k % GROUPS == 3 and k < SLABS - 1:
                 quantise_half(k // GROUPS + 1, 0)
             if k % GROUPS == 0:
                 quantise_half(k // GROUPS, 1)
+            if k >= 3 and on_gpsimd:
+                normalise_on_gpsimd(k - 3)
             project(k)
-            minus_mean(k - 2)
+            if k % 2 == 0 or k == SLABS - 1:
+                minus_mean(k - 2)
             add_residual(k - 1)
-            if k >= 3 and on_vector:
-                normalise_on_vector(k - 3)
         deviation(SLABS - 2)
         invert_deviation(SLABS - 2)
         add_residual(SLABS - 1)

@@ -18,11 +18,11 @@ CHANNELS = 512
 GROUPS = CHANNELS // P
 PACK = 4
 BANK = 512
+QUARTER = FRAMES // 4
 HALVES = FRAMES // BANK
 EPS = 1e-5
 SLABS = SEQS * GROUPS
-VECTOR_COLS = 0
-DRAIN_VECTOR_COLS = 640
+GPSIMD_COLS = 640
 
 FLOPS = 2 * SEQS * FRAMES * CHANNELS * CHANNELS
 
@@ -44,15 +44,18 @@ def tile_transformerencoderblock_pa_kernel(tc, h_attn, x, masks, Wo, bo, out):
         x_view = x.rearrange("n (p a) t -> n p a t", a=GROUPS)
         out_view = out.rearrange("n (p a) t -> n p a t", a=GROUPS)
 
-        mask_rows = consts.tile([P, FRAMES], BF16)
-        nc.vector.memset(mask_rows[:].bitcast(U32), 0)
+        first_mask = consts.tile([P, FRAMES], BF16)
+        nc.vector.memset(first_mask[:].bitcast(U32), 0)
+        later_masks = consts.tile([P, FRAMES], BF16)
+        nc.vector.memset(later_masks[:].bitcast(U32), 0)
+        mask_rows = [(first_mask, 0), (later_masks, 0), (later_masks, 1)]
         ident = consts.tile([P, P], F32)
         make_identity(nc, ident[:])
         warm = consts.tile([P, 1], F32)
         eps = consts.tile([P, 1], F32)
         nc.gpsimd.memset(eps[:], EPS)
-        row_select = consts.tile([P, SEQS], BF16)
-        nc.vector.tensor_copy(out=row_select[:], in_=ident[:, :SEQS])
+        row_select = consts.tile([P, 2], BF16)
+        nc.vector.tensor_copy(out=row_select[:], in_=ident[:, :2])
         mask_sb = consts.tile([P, SEQS * FRAMES], BF16)
 
         w_sb = consts.tile([P, GROUPS * CHANNELS], BF16)
@@ -70,10 +73,10 @@ def tile_transformerencoderblock_pa_kernel(tc, h_attn, x, masks, Wo, bo, out):
                 in_=h_view[n][:, first : first + count, :],
             )
 
-        def load_weights(pair):
+        def load_weights(first, count):
+            cols = slice(first * CHANNELS, (first + count) * CHANNELS)
             nc.sync.dma_start(
-                out=w_sb[:, pair * 1024 : (pair + 1) * 1024],
-                in_=Wo.rearrange("(p a) c -> p (a c)", a=GROUPS)[:, pair * 1024 : (pair + 1) * 1024],
+                out=w_sb[:, cols], in_=Wo.rearrange("(p a) c -> p (a c)", a=GROUPS)[:, cols]
             )
 
         def load_residual(n, pair):
@@ -81,34 +84,38 @@ def tile_transformerencoderblock_pa_kernel(tc, h_attn, x, masks, Wo, bo, out):
             nc.sync.dma_start(out=x_sb[n][:, groups, :], in_=x_view[n][:, groups, :])
 
         mask_view = masks.rearrange("n o t -> (n o) t")
-        nc.scalar.dma_start(out=mask_rows[0:1, :], in_=mask_view[0:1, :])
-        nc.scalar.dma_start(out=mask_rows[1:SEQS, :], in_=mask_view[1:SEQS, :])
         nc.scalar.dma_start(out=bo_sb[:], in_=bo.rearrange("(p a) -> p a", a=GROUPS))
-        load_weights(0)
+        load_weights(0, 1)
         load_frames(0, 0, 1)
+        nc.sync.dma_start(out=first_mask[0:1, :], in_=mask_view[0:1, :])
+        load_weights(1, 1)
         load_frames(0, 1, 1)
         load_frames(0, 2, 2)
-        load_weights(1)
+        load_weights(2, 2)
         load_frames(1, 0, 2)
         load_residual(0, 0)
+        nc.sync.dma_start(out=later_masks[0:2, :], in_=mask_view[1:3, :])
         load_frames(1, 2, 2)
-        load_frames(2, 0, 2)
         load_residual(0, 1)
+        load_frames(2, 0, 2)
+        load_residual(1, 0)
+        load_residual(1, 1)
         load_frames(2, 2, 2)
-        for n in range(1, SEQS):
-            nc.sync.dma_start(out=x_sb[n][:], in_=x_view[n])
+        load_residual(2, 0)
+        load_residual(2, 1)
 
         nc.scalar.activation(
             out=warm[:], in_=eps[:], func=ACT.Abs_reciprocal_sqrt, bias=eps[:], scale=1.0
         )
 
         def broadcast_mask(n, halves=(0, 1)):
+            mask_tile, row = mask_rows[n]
             mask_ps = transposed_psum.tile([P, FRAMES], BF16, tag="transposed")
             for half in halves:
                 nc.tensor.matmul(
                     out=mask_ps[:, half * BANK : (half + 1) * BANK],
-                    lhsT=row_select[:, n : n + 1].to_broadcast([P, P]),
-                    rhs=mask_rows[:, half * BANK : (half + 1) * BANK],
+                    lhsT=row_select[:, row : row + 1].to_broadcast([P, P]),
+                    rhs=mask_tile[:, half * BANK : (half + 1) * BANK],
                     start=True,
                     stop=True,
                 )
@@ -123,25 +130,25 @@ def tile_transformerencoderblock_pa_kernel(tc, h_attn, x, masks, Wo, bo, out):
         w_codes = consts.tile([P, GROUPS * P], U32, align_bytes=64)
         w_scales = consts.tile([P, GROUPS * P], U8, align_bytes=64)
 
-        def transpose_weights(pair):
-            w_ps = transposed_psum.tile([P, 2, 2, P], F32, tag="transposed")
-            for a2 in range(2):
+        def transpose_weights(first, count):
+            w_ps = transposed_psum.tile([P, count, 2, P], F32, tag="transposed")
+            for i in range(count):
                 for u in range(2):
-                    row = (2 * pair + a2) * 256
+                    row = (first + i) * CHANNELS // 2
                     nc.tensor.transpose(
-                        w_ps[:, a2, u, :], w_words[:, row + u : row + 256 : 2], ident[:]
+                        w_ps[:, i, u, :], w_words[:, row + u : row + CHANNELS // 2 : 2], ident[:]
                     )
-            regrouped = w_grouped_words[:, pair * BANK : (pair + 1) * BANK].rearrange(
-                "q (a p u) -> q a p u", a=2, u=2
+            regrouped = w_grouped_words[:, first * 2 * P : (first + count) * 2 * P].rearrange(
+                "q (a p u) -> q a p u", a=count, u=2
             )
             nc.scalar.copy(out=regrouped, in_=w_ps[:].rearrange("q a u p -> q a p u"))
 
-        def quantise_weights(pair):
-            cols = slice(2 * pair * P, (2 * pair + 2) * P)
+        def quantise_weights(first, count):
+            cols = slice(first * P, (first + count) * P)
             nc.vector.quantize_mx(
                 out=w_codes[:, cols].bitcast(FP8X4),
                 scales=w_scales[:, cols],
-                in_=w_grouped[:, pair * 1024 : (pair + 1) * 1024],
+                in_=w_grouped[:, first * P * PACK : (first + count) * P * PACK],
             )
 
         frames = {}
@@ -168,13 +175,17 @@ def tile_transformerencoderblock_pa_kernel(tc, h_attn, x, masks, Wo, bo, out):
             else:
                 nc.scalar.copy(out=regrouped, in_=h_ps[:].rearrange("q i u r -> q r i u"))
 
-        def quantise_half(n, half):
+        def quantise_frames(n, first, count):
             h_grouped, h_codes, h_scales = frames[n]
+            begin, end = first * QUARTER, (first + count) * QUARTER
             nc.vector.quantize_mx(
-                out=h_codes[:, half * BANK : (half + 1) * BANK].bitcast(FP8X4),
-                scales=h_scales[:, half * BANK : (half + 1) * BANK],
-                in_=h_grouped[:, half * BANK * PACK : (half + 1) * BANK * PACK],
+                out=h_codes[:, begin:end].bitcast(FP8X4),
+                scales=h_scales[:, begin:end],
+                in_=h_grouped[:, begin * PACK : end * PACK],
             )
+
+        def quantise_half(n, half):
+            quantise_frames(n, 2 * half, 2)
 
         projected = {}
         summed = {}
@@ -183,32 +194,30 @@ def tile_transformerencoderblock_pa_kernel(tc, h_attn, x, masks, Wo, bo, out):
         shifts = {}
         minus_means = {}
 
-        def project(k, halves=(0, 1)):
+        def project(k, begin, width):
             n, a = divmod(k, GROUPS)
             h_codes, h_scales = frames[n][1:]
-            if halves[0] == 0:
+            if begin == 0:
                 projected[k] = scratch.tile([P, FRAMES], F32, name="masked")
-            masked = projected[k]
-            for half in halves:
-                cols = slice(half * BANK, (half + 1) * BANK)
-                product = product_psum.tile([P, BANK], F32)
-                nc.tensor.matmul_mx(
-                    out=product[:],
-                    lhsT=w_codes[:, a * P : (a + 1) * P].bitcast(FP8X4),
-                    lhsT_scale=w_scales[:, a * P : (a + 1) * P],
-                    rhs=h_codes[:, cols].bitcast(FP8X4),
-                    rhs_scale=h_scales[:, cols],
-                    start=True,
-                    stop=True,
-                )
-                nc.vector.scalar_tensor_tensor(
-                    out=masked[:, cols],
-                    in0=product[:],
-                    scalar=bias_f32[:, a : a + 1],
-                    in1=mask_sb[:, n * FRAMES + half * BANK : n * FRAMES + (half + 1) * BANK],
-                    op0=ALU.add,
-                    op1=ALU.mult,
-                )
+            product = product_psum.tile([P, BANK], F32)
+            cols = slice(begin, begin + width)
+            nc.tensor.matmul_mx(
+                out=product[:, :width],
+                lhsT=w_codes[:, a * P : (a + 1) * P].bitcast(FP8X4),
+                lhsT_scale=w_scales[:, a * P : (a + 1) * P],
+                rhs=h_codes[:, cols].bitcast(FP8X4),
+                rhs_scale=h_scales[:, cols],
+                start=True,
+                stop=True,
+            )
+            nc.vector.scalar_tensor_tensor(
+                out=projected[k][:, cols],
+                in0=product[:, :width],
+                scalar=bias_f32[:, a : a + 1],
+                in1=mask_sb[:, n * FRAMES + begin : n * FRAMES + begin + width],
+                op0=ALU.add,
+                op1=ALU.mult,
+            )
 
         def add_residual(k):
             n, a = divmod(k, GROUPS)
@@ -250,29 +259,22 @@ def tile_transformerencoderblock_pa_kernel(tc, h_attn, x, masks, Wo, bo, out):
 
         def shift_mean(k):
             shift = stats.tile([P, 1], F32)
-            nc.scalar.activation(
-                out=shift[:], in_=minus_means[k][:], func=ACT.Identity, scale=inverted[k][:]
-            )
-            shifts[k] = shift
-
-        def normalise_on_scalar(k):
-            normed = slabs.tile([P, FRAMES], F32)
-            nc.scalar.activation(
-                out=normed[:], in_=summed[k][0][:], func=ACT.Identity,
-                bias=shifts[k][:], scale=inverted[k][:],
-            )
-            store(k, slice(0, FRAMES), normed)
-
-        def normalise_on_gpsimd(k):
-            shift = stats.tile([P, 1], F32)
             nc.vector.tensor_scalar(
                 out=shift[:], in0=summed[k][1][:], scalar1=inverted[k][:], scalar2=-1.0 / FRAMES,
                 op0=ALU.mult, op1=ALU.mult,
             )
+            shifts[k] = shift
+
+        def normalise_beside_vector(k):
             normed = slabs.tile([P, FRAMES], F32)
+            y = summed[k][0]
             nc.gpsimd.tensor_scalar(
-                out=normed[:], in0=summed[k][0][:], scalar1=inverted[k][:], scalar2=shift[:],
-                op0=ALU.mult, op1=ALU.add,
+                out=normed[:, :GPSIMD_COLS], in0=y[:, :GPSIMD_COLS], scalar1=inverted[k][:],
+                scalar2=shifts[k][:], op0=ALU.mult, op1=ALU.add,
+            )
+            nc.scalar.activation(
+                out=normed[:, GPSIMD_COLS:], in_=y[:, GPSIMD_COLS:], func=ACT.Identity,
+                bias=shifts[k][:], scale=inverted[k][:],
             )
             store(k, slice(0, FRAMES), normed)
 
@@ -297,54 +299,51 @@ def tile_transformerencoderblock_pa_kernel(tc, h_attn, x, masks, Wo, bo, out):
         bias_f32 = consts.tile([P, GROUPS], F32)
         nc.gpsimd.tensor_copy(out=bias_f32[:], in_=bo_sb[:])
 
-        transpose_weights(0)
+        transpose_weights(0, 1)
         transpose_quarter(0, 0, on_vector=True)
-        transpose_quarter(0, 1)
-        quantise_weights(0)
-        quantise_half(0, 0)
+        transpose_weights(1, 1)
         broadcast_mask(0, (0,))
+        transpose_quarter(0, 1)
+        quantise_weights(0, 1)
+        quantise_frames(0, 0, 1)
+        quantise_weights(1, 1)
+        project(0, 0, QUARTER)
         transpose_quarter(0, 2)
         transpose_quarter(0, 3)
-        project(0, (0,))
-        project(1, (0,))
+        quantise_frames(0, 1, 1)
+        project(1, 0, QUARTER)
+        project(0, QUARTER, QUARTER)
         broadcast_mask(0, (1,))
-        transpose_weights(1)
+        transpose_weights(2, 2)
         transpose_quarter(1, 0)
+        quantise_frames(0, 2, 2)
+        project(1, QUARTER, QUARTER)
+        quantise_weights(2, 2)
+        project(0, BANK, BANK)
         transpose_quarter(1, 1)
-        quantise_half(0, 1)
-        quantise_weights(1)
-        project(0, (1,))
-        project(1, (1,))
+        project(1, BANK, BANK)
         add_residual(0)
 
         for k in range(2, SLABS):
-            if k <= 4:
-                n, half = divmod(k + 1, HALVES)
-                transpose_quarter(n, 2 * half)
-                transpose_quarter(n, 2 * half + 1)
-            if k == 2:
-                broadcast_mask(1)
-            if k == 5:
-                broadcast_mask(2)
+            if k <= 7:
+                transpose_quarter(*divmod(k + 4, 4))
+            if k % GROUPS == 3 and k < SLABS - 1:
+                broadcast_mask(k // GROUPS + 1)
             deviation(k - 2)
-            on_gpsimd = (k - 3) % 2 == 1
-            if k >= 3 and not on_gpsimd:
-                shift_mean(k - 3)
-            invert_deviation(k - 2)
-            if k >= 3 and not on_gpsimd:
-                normalise_on_scalar(k - 3)
             if k % GROUPS == 3 and k < SLABS - 1:
                 quantise_half(k // GROUPS + 1, 0)
             if k % GROUPS == 0:
                 quantise_half(k // GROUPS, 1)
-            if k >= 3 and on_gpsimd:
-                normalise_on_gpsimd(k - 3)
-            project(k)
-            if k % 2 == 0 or k == SLABS - 1:
-                minus_mean(k - 2)
+            if k >= 3:
+                shift_mean(k - 3)
+                normalise_beside_vector(k - 3)
+            invert_deviation(k - 2)
+            project(k, 0, BANK)
+            project(k, BANK, BANK)
             add_residual(k - 1)
         deviation(SLABS - 2)
         invert_deviation(SLABS - 2)
+        minus_mean(SLABS - 3)
         add_residual(SLABS - 1)
         deviation(SLABS - 1)
         invert_deviation(SLABS - 1)

@@ -44,6 +44,8 @@ def tile_transformerencoderblock_pa_kernel(tc, h_attn, x, masks, Wo, bo, out):
         x_view = x.rearrange("n (p a) t -> n p a t", a=GROUPS)
         out_view = out.rearrange("n (p a) t -> n p a t", a=GROUPS)
 
+        zeros = consts.tile([P, 2 * P], F32)
+        nc.vector.memset(zeros[:], 0.0)
         first_mask = consts.tile([P, FRAMES], BF16)
         nc.vector.memset(first_mask[:].bitcast(U32), 0)
         later_masks = consts.tile([P, FRAMES], BF16)
@@ -90,11 +92,11 @@ def tile_transformerencoderblock_pa_kernel(tc, h_attn, x, masks, Wo, bo, out):
         nc.sync.dma_start(out=first_mask[0:1, :], in_=mask_view[0:1, :])
         load_weights(1, 1)
         load_frames(0, 1, 1)
+        nc.sync.dma_start(out=later_masks[0:2, :], in_=mask_view[1:3, :])
         load_frames(0, 2, 2)
         load_weights(2, 2)
         load_frames(1, 0, 2)
         load_residual(0, 0)
-        nc.sync.dma_start(out=later_masks[0:2, :], in_=mask_view[1:3, :])
         load_frames(1, 2, 2)
         load_residual(0, 1)
         load_frames(2, 0, 2)
@@ -108,7 +110,13 @@ def tile_transformerencoderblock_pa_kernel(tc, h_attn, x, masks, Wo, bo, out):
             out=warm[:], in_=eps[:], func=ACT.Abs_reciprocal_sqrt, bias=eps[:], scale=1.0
         )
 
-        def broadcast_mask(n, halves=(0, 1)):
+        def keep_busy(cols):
+            idle_ps = product_psum.tile([P, BANK], F32, tag="product")
+            nc.tensor.matmul(
+                out=idle_ps[:, :cols], lhsT=zeros[:, :P], rhs=zeros[:, :cols], start=True, stop=True
+            )
+
+        def spread_mask(n, halves=(0, 1)):
             mask_tile, row = mask_rows[n]
             mask_ps = transposed_psum.tile([P, FRAMES], BF16, tag="transposed")
             for half in halves:
@@ -119,6 +127,9 @@ def tile_transformerencoderblock_pa_kernel(tc, h_attn, x, masks, Wo, bo, out):
                     start=True,
                     stop=True,
                 )
+            return mask_ps
+
+        def keep_mask(n, mask_ps, halves=(0, 1)):
             first, end = halves[0] * BANK, (halves[-1] + 1) * BANK
             nc.scalar.copy(
                 out=mask_sb[:, n * FRAMES + first : n * FRAMES + end], in_=mask_ps[:, first:end]
@@ -199,7 +210,7 @@ def tile_transformerencoderblock_pa_kernel(tc, h_attn, x, masks, Wo, bo, out):
             h_codes, h_scales = frames[n][1:]
             if begin == 0:
                 projected[k] = scratch.tile([P, FRAMES], F32, name="masked")
-            product = product_psum.tile([P, BANK], F32)
+            product = product_psum.tile([P, BANK], F32, tag="product")
             cols = slice(begin, begin + width)
             nc.tensor.matmul_mx(
                 out=product[:, :width],
@@ -299,36 +310,43 @@ def tile_transformerencoderblock_pa_kernel(tc, h_attn, x, masks, Wo, bo, out):
         bias_f32 = consts.tile([P, GROUPS], F32)
         nc.gpsimd.tensor_copy(out=bias_f32[:], in_=bo_sb[:])
 
+        keep_busy(2 * P)
+        keep_busy(2 * P)
         transpose_weights(0, 1)
+        quantise_weights(0, 1)
         transpose_quarter(0, 0, on_vector=True)
         transpose_weights(1, 1)
-        broadcast_mask(0, (0,))
+        mask_ps = spread_mask(0, (0,))
+        keep_mask(0, mask_ps, (0,))
+        keep_busy(P)
         transpose_quarter(0, 1)
-        quantise_weights(0, 1)
         quantise_frames(0, 0, 1)
         quantise_weights(1, 1)
         project(0, 0, QUARTER)
+        mask_ps = spread_mask(0, (1,))
         transpose_quarter(0, 2)
         transpose_quarter(0, 3)
+        keep_mask(0, mask_ps, (1,))
         quantise_frames(0, 1, 1)
         project(1, 0, QUARTER)
         project(0, QUARTER, QUARTER)
-        broadcast_mask(0, (1,))
+        mask_ps = spread_mask(1)
         transpose_weights(2, 2)
-        transpose_quarter(1, 0)
+        keep_mask(1, mask_ps)
         quantise_frames(0, 2, 2)
         project(1, QUARTER, QUARTER)
         quantise_weights(2, 2)
         project(0, BANK, BANK)
-        transpose_quarter(1, 1)
+        mask_ps = spread_mask(2)
+        transpose_quarter(1, 0)
+        keep_mask(2, mask_ps)
         project(1, BANK, BANK)
+        transpose_quarter(1, 1)
         add_residual(0)
 
         for k in range(2, SLABS):
             if k <= 7:
                 transpose_quarter(*divmod(k + 4, 4))
-            if k % GROUPS == 3 and k < SLABS - 1:
-                broadcast_mask(k // GROUPS + 1)
             deviation(k - 2)
             if k % GROUPS == 3 and k < SLABS - 1:
                 quantise_half(k // GROUPS + 1, 0)

@@ -22,7 +22,7 @@ QUARTER = FRAMES // 4
 HALVES = FRAMES // BANK
 EPS = 1e-5
 SLABS = SEQS * GROUPS
-GPSIMD_COLS = 640
+GPSIMD_COLS = 384
 
 FLOPS = 2 * SEQS * FRAMES * CHANNELS * CHANNELS
 

@@ -23,6 +23,7 @@ HALVES = FRAMES // BANK
 EPS = 1e-5
 SLABS = SEQS * GROUPS
 GPSIMD_COLS = 384
+CATCH_UP = 9
 
 FLOPS = 2 * SEQS * FRAMES * CHANNELS * CHANNELS
 
@@ -34,8 +35,8 @@ def tile_transformerencoderblock_pa_kernel(tc, h_attn, x, masks, Wo, bo, out):
         inputs = ctx.enter_context(tc.tile_pool(name="inputs", bufs=1))
         quant = ctx.enter_context(tc.tile_pool(name="quant", bufs=SEQS))
         scratch = ctx.enter_context(tc.tile_pool(name="scratch", bufs=3))
-        slabs = ctx.enter_context(tc.tile_pool(name="slabs", bufs=4))
-        stats = ctx.enter_context(tc.tile_pool(name="stats", bufs=4))
+        slabs = ctx.enter_context(tc.tile_pool(name="slabs", bufs=6))
+        stats = ctx.enter_context(tc.tile_pool(name="stats", bufs=6))
         transposed_psum = ctx.enter_context(tc.psum_pool(name="transposed_psum", bufs=4))
         product_psum = ctx.enter_context(tc.psum_pool(name="product_psum", bufs=4))
         ctx.enter_context(tc.manual_schedule())
@@ -323,41 +324,57 @@ def tile_transformerencoderblock_pa_kernel(tc, h_attn, x, masks, Wo, bo, out):
         quantise_frames(0, 0, 1)
         quantise_weights(1, 1)
         project(0, 0, QUARTER)
-        mask_ps = spread_mask(0, (1,))
-        transpose_quarter(0, 2)
-        transpose_quarter(0, 3)
-        keep_mask(0, mask_ps, (1,))
-        quantise_frames(0, 1, 1)
         project(1, 0, QUARTER)
+        transpose_quarter(0, 2)
+        quantise_frames(0, 1, 1)
+        transpose_quarter(0, 3)
+        mask_ps = spread_mask(0, (1,))
+        keep_mask(0, mask_ps, (1,))
+        quantise_frames(0, 2, 1)
         project(0, QUARTER, QUARTER)
-        mask_ps = spread_mask(1)
-        transpose_weights(2, 2)
-        keep_mask(1, mask_ps)
-        quantise_frames(0, 2, 2)
         project(1, QUARTER, QUARTER)
-        quantise_weights(2, 2)
+        quantise_frames(0, 3, 1)
+        keep_busy(P)
+        transpose_weights(2, 2)
         project(0, BANK, BANK)
-        mask_ps = spread_mask(2)
-        transpose_quarter(1, 0)
-        keep_mask(2, mask_ps)
         project(1, BANK, BANK)
-        transpose_quarter(1, 1)
+        quantise_weights(2, 2)
+        transpose_quarter(1, 0)
+        mask_ps = spread_mask(1)
         add_residual(0)
+        project(2, 0, BANK)
+        project(2, BANK, BANK)
+        transpose_quarter(1, 1)
+        keep_mask(1, mask_ps)
+        deviation(0)
+        transpose_quarter(1, 2)
+        add_residual(1)
+        invert_deviation(0)
 
-        for k in range(2, SLABS):
+        for k in range(3, SLABS):
             if k <= 7:
                 transpose_quarter(*divmod(k + 4, 4))
             deviation(k - 2)
             if k % GROUPS == 3 and k < SLABS - 1:
                 quantise_half(k // GROUPS + 1, 0)
-            if k % GROUPS == 0:
-                quantise_half(k // GROUPS, 1)
-            if k >= 3:
-                shift_mean(k - 3)
-                normalise_beside_vector(k - 3)
+            if k < CATCH_UP:
+                ready = [k - 4] if k >= 4 else []
+            elif k == CATCH_UP:
+                ready = [k - 4, k - 3]
+            else:
+                ready = [k - 3]
+            for done in ready:
+                shift_mean(done)
+            for done in ready:
+                normalise_beside_vector(done)
             invert_deviation(k - 2)
             project(k, 0, BANK)
             project(k, BANK, BANK)
+            if k == 6:
+                mask_ps = spread_mask(2)
+                keep_mask(2, mask_ps)
+            if k % GROUPS == 3 and k < SLABS - 1:
+                quantise_half(k // GROUPS + 1, 1)
             add_residual(k - 1)
         deviation(SLABS - 2)
         invert_deviation(SLABS - 2)

@@ -317,9 +317,8 @@ def tile_transformerencoderblock_pa_kernel(tc, h_attn, x, masks, Wo, bo, out):
         quantise_weights(0, 1)
         transpose_quarter(0, 0, on_vector=True)
         transpose_weights(1, 1)
-        mask_ps = spread_mask(0, (0,))
-        keep_mask(0, mask_ps, (0,))
-        keep_busy(P)
+        mask_ps = spread_mask(0)
+        keep_mask(0, mask_ps)
         transpose_quarter(0, 1)
         quantise_frames(0, 0, 1)
         quantise_weights(1, 1)
@@ -328,28 +327,29 @@ def tile_transformerencoderblock_pa_kernel(tc, h_attn, x, masks, Wo, bo, out):
         transpose_quarter(0, 2)
         quantise_frames(0, 1, 1)
         transpose_quarter(0, 3)
-        mask_ps = spread_mask(0, (1,))
-        keep_mask(0, mask_ps, (1,))
+        keep_busy(P)
         quantise_frames(0, 2, 1)
         project(0, QUARTER, QUARTER)
         project(1, QUARTER, QUARTER)
         quantise_frames(0, 3, 1)
-        keep_busy(P)
+        project(0, 2 * QUARTER, QUARTER)
+        project(1, 2 * QUARTER, QUARTER)
+        project(0, 3 * QUARTER, QUARTER)
+        project(1, 3 * QUARTER, QUARTER)
         transpose_weights(2, 2)
-        project(0, BANK, BANK)
-        project(1, BANK, BANK)
-        quantise_weights(2, 2)
         transpose_quarter(1, 0)
-        mask_ps = spread_mask(1)
+        transpose_quarter(1, 1)
         add_residual(0)
+        quantise_weights(2, 2)
+        add_residual(1)
+        transpose_quarter(1, 2)
+        deviation(0)
         project(2, 0, BANK)
         project(2, BANK, BANK)
-        transpose_quarter(1, 1)
+        mask_ps = spread_mask(1)
         keep_mask(1, mask_ps)
-        deviation(0)
-        transpose_quarter(1, 2)
-        add_residual(1)
         invert_deviation(0)
+
 
         for k in range(3, SLABS):
             if k <= 7:
@@ -357,6 +357,8 @@ def tile_transformerencoderblock_pa_kernel(tc, h_attn, x, masks, Wo, bo, out):
             deviation(k - 2)
             if k % GROUPS == 3 and k < SLABS - 1:
                 quantise_half(k // GROUPS + 1, 0)
+            if k >= 8:
+                invert_deviation(k - 2)
             if k < CATCH_UP:
                 ready = [k - 4] if k >= 4 else []
             elif k == CATCH_UP:
@@ -367,7 +369,8 @@ def tile_transformerencoderblock_pa_kernel(tc, h_attn, x, masks, Wo, bo, out):
                 shift_mean(done)
             for done in ready:
                 normalise_beside_vector(done)
-            invert_deviation(k - 2)
+            if k < 8:
+                invert_deviation(k - 2)
             project(k, 0, BANK)
             project(k, BANK, BANK)
             if k == 6:

@@ -297,16 +297,74 @@ def tile_transformerencoderblock_pa_kernel(tc, h_attn, x, masks, Wo, bo, out):
                 op0=ALU.mult,
             )
 
-        def normalise_on_vector(k, pieces=1):
-            normed = slabs.tile([P, FRAMES], F32)
-            width = FRAMES // pieces
-            for i in range(pieces):
-                cols = slice(i * width, (i + 1) * width)
-                nc.vector.tensor_scalar(
-                    out=normed[:, cols], in0=summed[k][0][:, cols], scalar1=minus_means[k][:],
-                    scalar2=inverted[k][:], op0=ALU.add, op1=ALU.mult,
-                )
-                store(k, cols, normed)
+        normalised = {}
+
+        def normalise_on_vector(k, begin=0, width=FRAMES):
+            if begin == 0:
+                normalised[k] = slabs.tile([P, FRAMES], F32, name="normed")
+            cols = slice(begin, begin + width)
+            nc.vector.tensor_scalar(
+                out=normalised[k][:, cols], in0=summed[k][0][:, cols], scalar1=minus_means[k][:],
+                scalar2=inverted[k][:], op0=ALU.add, op1=ALU.mult,
+            )
+            store(k, cols, normalised[k])
+
+        def add_half(k, half):
+            n, a = divmod(k, GROUPS)
+            cols = slice(half * BANK, (half + 1) * BANK)
+            if half == 0:
+                last["y"] = slabs.tile([P, FRAMES], F32, name="y")
+            last["sum", half] = stats.tile([P, 1], F32, name="half_sum")
+            nc.vector.scalar_tensor_tensor(
+                out=last["y"][:, cols], in0=projected[k][:, cols], scalar=1.0,
+                in1=x_sb[n][:, a, cols], op0=ALU.mult, op1=ALU.add,
+                accum_out=last["sum", half][:],
+            )
+
+        def deviation_half(half):
+            cols = slice(half * BANK, (half + 1) * BANK)
+            squares = scratch.tile([P, FRAMES], BF16)
+            last["dev", half] = stats.tile([P, 1], F32, name="half_dev")
+            nc.scalar.activation(
+                out=squares[:, cols], in_=last["y"][:, cols], func=ACT.Square,
+                bias=last["sum", 0][:], scale=-float(BANK), accum_out=last["dev", half][:],
+            )
+
+        def last_statistics_early():
+            sums = last["sum", 0], last["sum", 1]
+            last["off"] = stats.tile([P, 1], F32, name="off")
+            nc.vector.tensor_scalar(
+                out=last["off"][:], in0=sums[1][:], scalar1=sums[0][:], scalar2=1.0 / FRAMES,
+                op0=ALU.subtract, op1=ALU.mult,
+            )
+            last["minus_mean"] = stats.tile([P, 1], F32, name="last_minus_mean")
+            nc.vector.tensor_scalar(
+                out=last["minus_mean"][:], in0=sums[0][:], scalar1=sums[1][:],
+                scalar2=-1.0 / FRAMES, op0=ALU.add, op1=ALU.mult,
+            )
+
+        def first_part():
+            last["part"] = stats.tile([P, 1], F32, name="first_part")
+            nc.vector.tensor_scalar(
+                out=last["part"][:], in0=last["dev", 0][:], scalar1=1.0 / (BANK**2 * FRAMES),
+                scalar2=EPS, op0=ALU.mult, op1=ALU.add,
+            )
+
+        def minus_rest():
+            last["rest"] = stats.tile([P, 1], F32, name="minus_rest")
+            nc.vector.scalar_tensor_tensor(
+                out=last["rest"][:], in0=last["off"][:], scalar=last["off"][:],
+                in1=last["part"][:], op0=ALU.mult, op1=ALU.subtract,
+            )
+
+        def invert_last():
+            last["rstd"] = stats.tile([P, 1], F32, name="last_rstd")
+            nc.scalar.activation(
+                out=last["rstd"][:], in_=last["dev", 1][:], func=ACT.Abs_reciprocal_sqrt,
+                bias=last["rest"][:], scale=-1.0 / (BANK**2 * FRAMES),
+            )
+
+        last = {}
 
         bias_f32 = consts.tile([P, GROUPS], F32)
         nc.gpsimd.tensor_copy(out=bias_f32[:], in_=bo_sb[:])
@@ -351,7 +409,7 @@ def tile_transformerencoderblock_pa_kernel(tc, h_attn, x, masks, Wo, bo, out):
         invert_deviation(0)
 
 
-        for k in range(3, SLABS):
+        for k in range(3, SLABS - 1):
             if k <= 7:
                 transpose_quarter(*divmod(k + 4, 4))
             deviation(k - 2)
@@ -379,14 +437,32 @@ def tile_transformerencoderblock_pa_kernel(tc, h_attn, x, masks, Wo, bo, out):
             if k % GROUPS == 3 and k < SLABS - 1:
                 quantise_half(k // GROUPS + 1, 1)
             add_residual(k - 1)
-        deviation(SLABS - 2)
-        invert_deviation(SLABS - 2)
-        minus_mean(SLABS - 3)
-        add_residual(SLABS - 1)
-        deviation(SLABS - 1)
-        invert_deviation(SLABS - 1)
-        minus_mean(SLABS - 2)
-        normalise_on_vector(SLABS - 3)
-        minus_mean(SLABS - 1)
-        normalise_on_vector(SLABS - 2)
-        normalise_on_vector(SLABS - 1, pieces=2)
+
+        k = SLABS - 1
+        deviation(k - 2)
+        invert_deviation(k - 2)
+        add_residual(k - 1)
+        minus_mean(k - 2)
+        shift_mean(k - 3)
+        normalise_beside_vector(k - 3)
+        project(k, 0, BANK)
+        project(k, BANK, BANK)
+        deviation(k - 1)
+        invert_deviation(k - 1)
+        minus_mean(k - 1)
+        normalise_on_vector(k - 2)
+        add_half(k, 0)
+        deviation_half(0)
+        add_half(k, 1)
+        deviation_half(1)
+        normalise_on_vector(k - 1, 0, BANK)
+        last_statistics_early()
+        normalise_on_vector(k - 1, BANK, BANK)
+        first_part()
+        minus_rest()
+        invert_last()
+        summed[k] = (last["y"], None)
+        minus_means[k] = last["minus_mean"]
+        inverted[k] = last["rstd"]
+        normalise_on_vector(k, 0, BANK)
+        normalise_on_vector(k, BANK, BANK)

@@ -22,8 +22,7 @@ QUARTER = FRAMES // 4
 HALVES = FRAMES // BANK
 EPS = 1e-5
 SLABS = SEQS * GROUPS
-GPSIMD_COLS = 384
-CATCH_UP = 9
+GPSIMD_COLS = 512
 
 FLOPS = 2 * SEQS * FRAMES * CHANNELS * CHANNELS
 
@@ -34,7 +33,7 @@ def tile_transformerencoderblock_pa_kernel(tc, h_attn, x, masks, Wo, bo, out):
         consts = ctx.enter_context(tc.tile_pool(name="consts", bufs=1))
         inputs = ctx.enter_context(tc.tile_pool(name="inputs", bufs=1))
         quant = ctx.enter_context(tc.tile_pool(name="quant", bufs=SEQS))
-        scratch = ctx.enter_context(tc.tile_pool(name="scratch", bufs=3))
+        scratch = ctx.enter_context(tc.tile_pool(name="scratch", bufs=5))
         slabs = ctx.enter_context(tc.tile_pool(name="slabs", bufs=6))
         stats = ctx.enter_context(tc.tile_pool(name="stats", bufs=6))
         transposed_psum = ctx.enter_context(tc.psum_pool(name="transposed_psum", bufs=4))
@@ -210,7 +209,7 @@ def tile_transformerencoderblock_pa_kernel(tc, h_attn, x, masks, Wo, bo, out):
             n, a = divmod(k, GROUPS)
             h_codes, h_scales = frames[n][1:]
             if begin == 0:
-                projected[k] = scratch.tile([P, FRAMES], F32, name="masked")
+                projected[k] = scratch.tile([P, FRAMES], F32, name="masked", tag="masked")
             product = product_psum.tile([P, BANK], F32, tag="product")
             cols = slice(begin, begin + width)
             nc.tensor.matmul_mx(
@@ -269,20 +268,25 @@ def tile_transformerencoderblock_pa_kernel(tc, h_attn, x, masks, Wo, bo, out):
             n, a = divmod(k, GROUPS)
             nc.sync.dma_start(out=out_view[n][:, a, cols], in_=normed[:, cols])
 
+        def scalar_minus_mean(k):
+            minus_means[k] = stats.tile([P, 1], F32, name="minus_mean")
+            nc.scalar.activation(
+                out=minus_means[k][:], in_=summed[k][1][:], func=ACT.Copy, scale=-1.0 / FRAMES,
+            )
+
         def shift_mean(k):
             shift = stats.tile([P, 1], F32)
-            nc.vector.tensor_scalar(
-                out=shift[:], in0=summed[k][1][:], scalar1=inverted[k][:], scalar2=-1.0 / FRAMES,
-                op0=ALU.mult, op1=ALU.mult,
+            nc.scalar.activation(
+                out=shift[:], in_=minus_means[k][:], func=ACT.Copy, scale=inverted[k][:],
             )
             shifts[k] = shift
 
         def normalise_beside_vector(k):
-            normed = slabs.tile([P, FRAMES], F32)
+            normed = scratch.tile([P, FRAMES], F32, name="normed", tag="masked")
             y = summed[k][0]
             nc.gpsimd.tensor_scalar(
-                out=normed[:, :GPSIMD_COLS], in0=y[:, :GPSIMD_COLS], scalar1=inverted[k][:],
-                scalar2=shifts[k][:], op0=ALU.mult, op1=ALU.add,
+                out=normed[:, :GPSIMD_COLS], in0=y[:, :GPSIMD_COLS], scalar1=minus_means[k][:],
+                scalar2=inverted[k][:], op0=ALU.add, op1=ALU.mult,
             )
             nc.scalar.activation(
                 out=normed[:, GPSIMD_COLS:], in_=y[:, GPSIMD_COLS:], func=ACT.Identity,
@@ -406,30 +410,21 @@ def tile_transformerencoderblock_pa_kernel(tc, h_attn, x, masks, Wo, bo, out):
         project(2, BANK, BANK)
         mask_ps = spread_mask(1)
         keep_mask(1, mask_ps)
+        scalar_minus_mean(0)
         invert_deviation(0)
 
 
         for k in range(3, SLABS - 1):
             if k <= 7:
                 transpose_quarter(*divmod(k + 4, 4))
+            shift_mean(k - 3)
             deviation(k - 2)
             if k % GROUPS == 3 and k < SLABS - 1:
                 quantise_half(k // GROUPS + 1, 0)
-            if k >= 8:
-                invert_deviation(k - 2)
-            if k < CATCH_UP:
-                ready = [k - 4] if k >= 4 else []
-            elif k == CATCH_UP:
-                ready = [k - 4, k - 3]
-            else:
-                ready = [k - 3]
-            for done in ready:
-                shift_mean(done)
-            for done in ready:
-                normalise_beside_vector(done)
-            if k < 8:
-                invert_deviation(k - 2)
+            scalar_minus_mean(k - 2)
             project(k, 0, BANK)
+            normalise_beside_vector(k - 3)
+            invert_deviation(k - 2)
             project(k, BANK, BANK)
             if k == 6:
                 mask_ps = spread_mask(2)
@@ -439,13 +434,13 @@ def tile_transformerencoderblock_pa_kernel(tc, h_attn, x, masks, Wo, bo, out):
             add_residual(k - 1)
 
         k = SLABS - 1
+        shift_mean(k - 3)
         deviation(k - 2)
         invert_deviation(k - 2)
         add_residual(k - 1)
         minus_mean(k - 2)
-        shift_mean(k - 3)
-        normalise_beside_vector(k - 3)
         project(k, 0, BANK)
+        normalise_beside_vector(k - 3)
         project(k, BANK, BANK)
         deviation(k - 1)
         invert_deviation(k - 1)

@@ -384,12 +384,11 @@ def tile_transformerencoderblock_pa_kernel(tc, h_attn, x, masks, Wo, bo, out):
         transpose_quarter(0, 1)
         quantise_frames(0, 0, 1)
         quantise_weights(1, 1)
-        project(0, 0, QUARTER)
-        project(1, 0, QUARTER)
         transpose_quarter(0, 2)
         quantise_frames(0, 1, 1)
+        project(0, 0, QUARTER)
+        project(1, 0, QUARTER)
         transpose_quarter(0, 3)
-        keep_busy(P)
         quantise_frames(0, 2, 1)
         project(0, QUARTER, QUARTER)
         project(1, QUARTER, QUARTER)
@@ -413,7 +412,6 @@ def tile_transformerencoderblock_pa_kernel(tc, h_attn, x, masks, Wo, bo, out):
         scalar_minus_mean(0)
         invert_deviation(0)
 
-
         for k in range(3, SLABS - 1):
             if k <= 7:
                 transpose_quarter(*divmod(k + 4, 4))
@@ -436,11 +434,11 @@ def tile_transformerencoderblock_pa_kernel(tc, h_attn, x, masks, Wo, bo, out):
         k = SLABS - 1
         shift_mean(k - 3)
         deviation(k - 2)
-        invert_deviation(k - 2)
         add_residual(k - 1)
         minus_mean(k - 2)
         project(k, 0, BANK)
         normalise_beside_vector(k - 3)
+        invert_deviation(k - 2)
         project(k, BANK, BANK)
         deviation(k - 1)
         invert_deviation(k - 1)
@@ -452,8 +450,8 @@ def tile_transformerencoderblock_pa_kernel(tc, h_attn, x, masks, Wo, bo, out):
         deviation_half(1)
         normalise_on_vector(k - 1, 0, BANK)
         last_statistics_early()
-        normalise_on_vector(k - 1, BANK, BANK)
         first_part()
+        normalise_on_vector(k - 1, BANK, BANK)
         minus_rest()
         invert_last()
         summed[k] = (last["y"], None)

@@ -209,7 +209,7 @@ def tile_transformerencoderblock_pa_kernel(tc, h_attn, x, masks, Wo, bo, out):
             n, a = divmod(k, GROUPS)
             h_codes, h_scales = frames[n][1:]
             if begin == 0:
-                projected[k] = scratch.tile([P, FRAMES], F32, name="masked", tag="masked")
+                projected[k] = scratch.tile([P, FRAMES], F32, name="masked")
             product = product_psum.tile([P, BANK], F32, tag="product")
             cols = slice(begin, begin + width)
             nc.tensor.matmul_mx(
@@ -282,7 +282,7 @@ def tile_transformerencoderblock_pa_kernel(tc, h_attn, x, masks, Wo, bo, out):
             shifts[k] = shift
 
         def normalise_beside_vector(k):
-            normed = scratch.tile([P, FRAMES], F32, name="normed", tag="masked")
+            normed = slabs.tile([P, FRAMES], F32, name="normed")
             y = summed[k][0]
             nc.gpsimd.tensor_scalar(
                 out=normed[:, :GPSIMD_COLS], in0=y[:, :GPSIMD_COLS], scalar1=minus_means[k][:],

@@ -22,7 +22,7 @@ QUARTER = FRAMES // 4
 HALVES = FRAMES // BANK
 EPS = 1e-5
 SLABS = SEQS * GROUPS
-GPSIMD_COLS = 512
+GPSIMD_COLS = 448
 
 FLOPS = 2 * SEQS * FRAMES * CHANNELS * CHANNELS
 

from contextlib import ExitStack

import concourse.mybir as mybir
from concourse.masks import make_identity

F32 = mybir.dt.float32
BF16 = mybir.dt.bfloat16
U32 = mybir.dt.uint32
U8 = mybir.dt.uint8
FP8X4 = mybir.dt.float8_e4m3fn_x4
ALU = mybir.AluOpType
ACT = mybir.ActivationFunctionType

P = 128
SEQS = 3
FRAMES = 1024
CHANNELS = 512
GROUPS = CHANNELS // P
PACK = 4
BANK = 512
QUARTER = FRAMES // 4
HALVES = FRAMES // BANK
EPS = 1e-5
SLABS = SEQS * GROUPS
GPSIMD_COLS = 448

FLOPS = 2 * SEQS * FRAMES * CHANNELS * CHANNELS


def tile_transformerencoderblock_pa_kernel(tc, h_attn, x, masks, Wo, bo, out):
    nc = tc.nc
    with ExitStack() as ctx:
        consts = ctx.enter_context(tc.tile_pool(name="consts", bufs=1))
        inputs = ctx.enter_context(tc.tile_pool(name="inputs", bufs=1))
        quant = ctx.enter_context(tc.tile_pool(name="quant", bufs=SEQS))
        scratch = ctx.enter_context(tc.tile_pool(name="scratch", bufs=5))
        slabs = ctx.enter_context(tc.tile_pool(name="slabs", bufs=6))
        stats = ctx.enter_context(tc.tile_pool(name="stats", bufs=6))
        transposed_psum = ctx.enter_context(tc.psum_pool(name="transposed_psum", bufs=4))
        product_psum = ctx.enter_context(tc.psum_pool(name="product_psum", bufs=4))
        ctx.enter_context(tc.manual_schedule())

        h_view = h_attn.rearrange("n (j r i) c -> n r j (i c)", r=P, i=2)
        x_view = x.rearrange("n (p a) t -> n p a t", a=GROUPS)
        out_view = out.rearrange("n (p a) t -> n p a t", a=GROUPS)

        zeros = consts.tile([P, 2 * P], F32)
        nc.vector.memset(zeros[:], 0.0)
        first_mask = consts.tile([P, FRAMES], BF16)
        nc.vector.memset(first_mask[:].bitcast(U32), 0)
        later_masks = consts.tile([P, FRAMES], BF16)
        nc.vector.memset(later_masks[:].bitcast(U32), 0)
        mask_rows = [(first_mask, 0), (later_masks, 0), (later_masks, 1)]
        ident = consts.tile([P, P], F32)
        make_identity(nc, ident[:])
        warm = consts.tile([P, 1], F32)
        eps = consts.tile([P, 1], F32)
        nc.gpsimd.memset(eps[:], EPS)
        row_select = consts.tile([P, 2], BF16)
        nc.vector.tensor_copy(out=row_select[:], in_=ident[:, :2])
        mask_sb = consts.tile([P, SEQS * FRAMES], BF16)

        w_sb = consts.tile([P, GROUPS * CHANNELS], BF16)
        bo_sb = consts.tile([P, GROUPS], BF16)
        h_sb = [
            inputs.tile([P, FRAMES * CHANNELS // P], BF16, name="h_sb%d" % n) for n in range(SEQS)
        ]
        x_sb = [inputs.tile([P, GROUPS, FRAMES], BF16, name="x_sb%d" % n) for n in range(SEQS)]

        def load_frames(n, first, count):
            nc.sync.dma_start(
                out=h_sb[n][:, first * 1024 : (first + count) * 1024].rearrange(
                    "r (j c) -> r j c", j=count
                ),
                in_=h_view[n][:, first : first + count, :],
            )

        def load_weights(first, count):
            cols = slice(first * CHANNELS, (first + count) * CHANNELS)
            nc.sync.dma_start(
                out=w_sb[:, cols], in_=Wo.rearrange("(p a) c -> p (a c)", a=GROUPS)[:, cols]
            )

        def load_residual(n, pair):
            groups = slice(2 * pair, 2 * pair + 2)
            nc.sync.dma_start(out=x_sb[n][:, groups, :], in_=x_view[n][:, groups, :])

        mask_view = masks.rearrange("n o t -> (n o) t")
        nc.scalar.dma_start(out=bo_sb[:], in_=bo.rearrange("(p a) -> p a", a=GROUPS))
        load_weights(0, 1)
        load_frames(0, 0, 1)
        nc.sync.dma_start(out=first_mask[0:1, :], in_=mask_view[0:1, :])
        load_weights(1, 1)
        load_frames(0, 1, 1)
        nc.sync.dma_start(out=later_masks[0:2, :], in_=mask_view[1:3, :])
        load_frames(0, 2, 2)
        load_weights(2, 2)
        load_frames(1, 0, 2)
        load_residual(0, 0)
        load_frames(1, 2, 2)
        load_residual(0, 1)
        load_frames(2, 0, 2)
        load_residual(1, 0)
        load_residual(1, 1)
        load_frames(2, 2, 2)
        load_residual(2, 0)
        load_residual(2, 1)

        nc.scalar.activation(
            out=warm[:], in_=eps[:], func=ACT.Abs_reciprocal_sqrt, bias=eps[:], scale=1.0
        )

        def keep_busy(cols):
            idle_ps = product_psum.tile([P, BANK], F32, tag="product")
            nc.tensor.matmul(
                out=idle_ps[:, :cols], lhsT=zeros[:, :P], rhs=zeros[:, :cols], start=True, stop=True
            )

        def spread_mask(n, halves=(0, 1)):
            mask_tile, row = mask_rows[n]
            mask_ps = transposed_psum.tile([P, FRAMES], BF16, tag="transposed")
            for half in halves:
                nc.tensor.matmul(
                    out=mask_ps[:, half * BANK : (half + 1) * BANK],
                    lhsT=row_select[:, row : row + 1].to_broadcast([P, P]),
                    rhs=mask_tile[:, half * BANK : (half + 1) * BANK],
                    start=True,
                    stop=True,
                )
            return mask_ps

        def keep_mask(n, mask_ps, halves=(0, 1)):
            first, end = halves[0] * BANK, (halves[-1] + 1) * BANK
            nc.scalar.copy(
                out=mask_sb[:, n * FRAMES + first : n * FRAMES + end], in_=mask_ps[:, first:end]
            )

        w_words = w_sb[:].bitcast(F32)
        w_grouped = consts.tile([P, GROUPS * P * PACK], BF16, align_bytes=64)
        w_grouped_words = w_grouped[:].bitcast(F32)
        w_codes = consts.tile([P, GROUPS * P], U32, align_bytes=64)
        w_scales = consts.tile([P, GROUPS * P], U8, align_bytes=64)

        def transpose_weights(first, count):
            w_ps = transposed_psum.tile([P, count, 2, P], F32, tag="transposed")
            for i in range(count):
                for u in range(2):
                    row = (first + i) * CHANNELS // 2
                    nc.tensor.transpose(
                        w_ps[:, i, u, :], w_words[:, row + u : row + CHANNELS // 2 : 2], ident[:]
                    )
            regrouped = w_grouped_words[:, first * 2 * P : (first + count) * 2 * P].rearrange(
                "q (a p u) -> q a p u", a=count, u=2
            )
            nc.scalar.copy(out=regrouped, in_=w_ps[:].rearrange("q a u p -> q a p u"))

        def quantise_weights(first, count):
            cols = slice(first * P, (first + count) * P)
            nc.vector.quantize_mx(
                out=w_codes[:, cols].bitcast(FP8X4),
                scales=w_scales[:, cols],
                in_=w_grouped[:, first * P * PACK : (first + count) * P * PACK],
            )

        frames = {}

        def transpose_quarter(n, j, on_vector=False):
            if j == 0:
                h_grouped = quant.tile([P, FRAMES * PACK], BF16, align_bytes=64)
                h_codes = quant.tile([P, FRAMES], U32, align_bytes=64)
                h_scales = quant.tile([P, FRAMES], U8, align_bytes=64)
                frames[n] = (h_grouped, h_codes, h_scales)
            h_words = h_sb[n][:].bitcast(F32)
            h_ps = transposed_psum.tile([P, 2, 2, P], F32, tag="transposed")
            for i in range(2):
                for u in range(2):
                    row = j * 512 + i * 256
                    nc.tensor.transpose(
                        h_ps[:, i, u, :], h_words[:, row + u : row + 256 : 2], ident[:]
                    )
            regrouped = frames[n][0][:].bitcast(F32)[:, j * BANK : (j + 1) * BANK].rearrange(
                "q (r i u) -> q r i u", i=2, u=2
            )
            if on_vector:
                nc.vector.tensor_copy(out=regrouped, in_=h_ps[:].rearrange("q i u r -> q r i u"))
            else:
                nc.scalar.copy(out=regrouped, in_=h_ps[:].rearrange("q i u r -> q r i u"))

        def quantise_frames(n, first, count):
            h_grouped, h_codes, h_scales = frames[n]
            begin, end = first * QUARTER, (first + count) * QUARTER
            nc.vector.quantize_mx(
                out=h_codes[:, begin:end].bitcast(FP8X4),
                scales=h_scales[:, begin:end],
                in_=h_grouped[:, begin * PACK : end * PACK],
            )

        def quantise_half(n, half):
            quantise_frames(n, 2 * half, 2)

        projected = {}
        summed = {}
        deviations = {}
        inverted = {}
        shifts = {}
        minus_means = {}

        def project(k, begin, width):
            n, a = divmod(k, GROUPS)
            h_codes, h_scales = frames[n][1:]
            if begin == 0:
                projected[k] = scratch.tile([P, FRAMES], F32, name="masked")
            product = product_psum.tile([P, BANK], F32, tag="product")
            cols = slice(begin, begin + width)
            nc.tensor.matmul_mx(
                out=product[:, :width],
                lhsT=w_codes[:, a * P : (a + 1) * P].bitcast(FP8X4),
                lhsT_scale=w_scales[:, a * P : (a + 1) * P],
                rhs=h_codes[:, cols].bitcast(FP8X4),
                rhs_scale=h_scales[:, cols],
                start=True,
                stop=True,
            )
            nc.vector.scalar_tensor_tensor(
                out=projected[k][:, cols],
                in0=product[:, :width],
                scalar=bias_f32[:, a : a + 1],
                in1=mask_sb[:, n * FRAMES + begin : n * FRAMES + begin + width],
                op0=ALU.add,
                op1=ALU.mult,
            )

        def add_residual(k):
            n, a = divmod(k, GROUPS)
            masked = projected[k]
            y = slabs.tile([P, FRAMES], F32)
            y_sum = stats.tile([P, 1], F32)
            nc.vector.scalar_tensor_tensor(
                out=y[:],
                in0=masked[:],
                scalar=1.0,
                in1=x_sb[n][:, a, :],
                op0=ALU.mult,
                op1=ALU.add,
                accum_out=y_sum[:],
            )
            summed[k] = (y, y_sum)

        def deviation(k):
            y, y_sum = summed[k]
            squares = scratch.tile([P, FRAMES], BF16)
            dev_sum = stats.tile([P, 1], F32)
            nc.scalar.activation(
                out=squares[:], in_=y[:], func=ACT.Square, bias=y_sum[:], scale=-float(FRAMES),
                accum_out=dev_sum[:],
            )
            deviations[k] = dev_sum

        def invert_deviation(k):
            rstd = stats.tile([P, 1], F32)
            nc.scalar.activation(
                out=rstd[:], in_=deviations[k][:], func=ACT.Abs_reciprocal_sqrt,
                bias=eps[:], scale=1.0 / FRAMES**3,
            )
            inverted[k] = rstd

        def store(k, cols, normed):
            n, a = divmod(k, GROUPS)
            nc.sync.dma_start(out=out_view[n][:, a, cols], in_=normed[:, cols])

        def scalar_minus_mean(k):
            minus_means[k] = stats.tile([P, 1], F32, name="minus_mean")
            nc.scalar.activation(
                out=minus_means[k][:], in_=summed[k][1][:], func=ACT.Copy, scale=-1.0 / FRAMES,
            )

        def shift_mean(k):
            shift = stats.tile([P, 1], F32)
            nc.scalar.activation(
                out=shift[:], in_=minus_means[k][:], func=ACT.Copy, scale=inverted[k][:],
            )
            shifts[k] = shift

        def normalise_beside_vector(k):
            normed = slabs.tile([P, FRAMES], F32, name="normed")
            y = summed[k][0]
            nc.gpsimd.tensor_scalar(
                out=normed[:, :GPSIMD_COLS], in0=y[:, :GPSIMD_COLS], scalar1=minus_means[k][:],
                scalar2=inverted[k][:], op0=ALU.add, op1=ALU.mult,
            )
            nc.scalar.activation(
                out=normed[:, GPSIMD_COLS:], in_=y[:, GPSIMD_COLS:], func=ACT.Identity,
                bias=shifts[k][:], scale=inverted[k][:],
            )
            store(k, slice(0, FRAMES), normed)

        def minus_mean(k):
            minus_means[k] = stats.tile([P, 1], F32, name="minus_mean")
            nc.vector.tensor_scalar(
                out=minus_means[k][:], in0=summed[k][1][:], scalar1=-1.0 / FRAMES, scalar2=None,
                op0=ALU.mult,
            )

        normalised = {}

        def normalise_on_vector(k, begin=0, width=FRAMES):
            if begin == 0:
                normalised[k] = slabs.tile([P, FRAMES], F32, name="normed")
            cols = slice(begin, begin + width)
            nc.vector.tensor_scalar(
                out=normalised[k][:, cols], in0=summed[k][0][:, cols], scalar1=minus_means[k][:],
                scalar2=inverted[k][:], op0=ALU.add, op1=ALU.mult,
            )
            store(k, cols, normalised[k])

        def add_half(k, half):
            n, a = divmod(k, GROUPS)
            cols = slice(half * BANK, (half + 1) * BANK)
            if half == 0:
                last["y"] = slabs.tile([P, FRAMES], F32, name="y")
            last["sum", half] = stats.tile([P, 1], F32, name="half_sum")
            nc.vector.scalar_tensor_tensor(
                out=last["y"][:, cols], in0=projected[k][:, cols], scalar=1.0,
                in1=x_sb[n][:, a, cols], op0=ALU.mult, op1=ALU.add,
                accum_out=last["sum", half][:],
            )

        def deviation_half(half):
            cols = slice(half * BANK, (half + 1) * BANK)
            squares = scratch.tile([P, FRAMES], BF16)
            last["dev", half] = stats.tile([P, 1], F32, name="half_dev")
            nc.scalar.activation(
                out=squares[:, cols], in_=last["y"][:, cols], func=ACT.Square,
                bias=last["sum", 0][:], scale=-float(BANK), accum_out=last["dev", half][:],
            )

        def last_statistics_early():
            sums = last["sum", 0], last["sum", 1]
            last["off"] = stats.tile([P, 1], F32, name="off")
            nc.vector.tensor_scalar(
                out=last["off"][:], in0=sums[1][:], scalar1=sums[0][:], scalar2=1.0 / FRAMES,
                op0=ALU.subtract, op1=ALU.mult,
            )
            last["minus_mean"] = stats.tile([P, 1], F32, name="last_minus_mean")
            nc.vector.tensor_scalar(
                out=last["minus_mean"][:], in0=sums[0][:], scalar1=sums[1][:],
                scalar2=-1.0 / FRAMES, op0=ALU.add, op1=ALU.mult,
            )

        def first_part():
            last["part"] = stats.tile([P, 1], F32, name="first_part")
            nc.vector.tensor_scalar(
                out=last["part"][:], in0=last["dev", 0][:], scalar1=1.0 / (BANK**2 * FRAMES),
                scalar2=EPS, op0=ALU.mult, op1=ALU.add,
            )

        def minus_rest():
            last["rest"] = stats.tile([P, 1], F32, name="minus_rest")
            nc.vector.scalar_tensor_tensor(
                out=last["rest"][:], in0=last["off"][:], scalar=last["off"][:],
                in1=last["part"][:], op0=ALU.mult, op1=ALU.subtract,
            )

        def invert_last():
            last["rstd"] = stats.tile([P, 1], F32, name="last_rstd")
            nc.scalar.activation(
                out=last["rstd"][:], in_=last["dev", 1][:], func=ACT.Abs_reciprocal_sqrt,
                bias=last["rest"][:], scale=-1.0 / (BANK**2 * FRAMES),
            )

        last = {}

        bias_f32 = consts.tile([P, GROUPS], F32)
        nc.gpsimd.tensor_copy(out=bias_f32[:], in_=bo_sb[:])

        keep_busy(2 * P)
        keep_busy(2 * P)
        transpose_weights(0, 1)
        quantise_weights(0, 1)
        transpose_quarter(0, 0, on_vector=True)
        transpose_weights(1, 1)
        mask_ps = spread_mask(0)
        keep_mask(0, mask_ps)
        transpose_quarter(0, 1)
        quantise_frames(0, 0, 1)
        quantise_weights(1, 1)
        transpose_quarter(0, 2)
        quantise_frames(0, 1, 1)
        project(0, 0, QUARTER)
        project(1, 0, QUARTER)
        transpose_quarter(0, 3)
        quantise_frames(0, 2, 1)
        project(0, QUARTER, QUARTER)
        project(1, QUARTER, QUARTER)
        quantise_frames(0, 3, 1)
        project(0, 2 * QUARTER, QUARTER)
        project(1, 2 * QUARTER, QUARTER)
        project(0, 3 * QUARTER, QUARTER)
        project(1, 3 * QUARTER, QUARTER)
        transpose_weights(2, 2)
        transpose_quarter(1, 0)
        transpose_quarter(1, 1)
        add_residual(0)
        quantise_weights(2, 2)
        add_residual(1)
        transpose_quarter(1, 2)
        deviation(0)
        project(2, 0, BANK)
        project(2, BANK, BANK)
        mask_ps = spread_mask(1)
        keep_mask(1, mask_ps)
        scalar_minus_mean(0)
        invert_deviation(0)

        for k in range(3, SLABS - 1):
            if k <= 7:
                transpose_quarter(*divmod(k + 4, 4))
            shift_mean(k - 3)
            deviation(k - 2)
            if k % GROUPS == 3 and k < SLABS - 1:
                quantise_half(k // GROUPS + 1, 0)
            scalar_minus_mean(k - 2)
            project(k, 0, BANK)
            normalise_beside_vector(k - 3)
            invert_deviation(k - 2)
            project(k, BANK, BANK)
            if k == 6:
                mask_ps = spread_mask(2)
                keep_mask(2, mask_ps)
            if k % GROUPS == 3 and k < SLABS - 1:
                quantise_half(k // GROUPS + 1, 1)
            add_residual(k - 1)

        k = SLABS - 1
        shift_mean(k - 3)
        deviation(k - 2)
        add_residual(k - 1)
        minus_mean(k - 2)
        project(k, 0, BANK)
        normalise_beside_vector(k - 3)
        invert_deviation(k - 2)
        project(k, BANK, BANK)
        deviation(k - 1)
        invert_deviation(k - 1)
        minus_mean(k - 1)
        normalise_on_vector(k - 2)
        add_half(k, 0)
        deviation_half(0)
        add_half(k, 1)
        deviation_half(1)
        normalise_on_vector(k - 1, 0, BANK)
        last_statistics_early()
        first_part()
        normalise_on_vector(k - 1, BANK, BANK)
        minus_rest()
        invert_last()
        summed[k] = (last["y"], None)
        minus_means[k] = last["minus_mean"]
        inverted[k] = last["rstd"]
        normalise_on_vector(k, 0, BANK)
        normalise_on_vector(k, BANK, BANK)
